import numpy as np
import ml_dtypes

BF16 = ml_dtypes.bfloat16


def bf(x):
    return np.asarray(x, np.float32).astype(BF16)


def f32(x):
    return np.asarray(x, np.float32)


def f64(x):
    return np.asarray(x).astype(np.float64)


def striped(idx):
    return np.tile(idx.reshape(-1, 16).T, (8, 1))


V, S, N, P = 256, 256, 256, 128
SCALE = 2.0


def softmax_rows(a):
    e = np.exp(a - a.max(axis=1, keepdims=True))
    return e / e.sum(axis=1, keepdims=True)


def setup_inputs():
    return {"logits": f32(SCALE * np.random.standard_normal((V, S))), "offs": striped(np.random.permutation(S)[:N])}


def reference(logits, offs):
    idx = offs[:16].T.reshape(-1)
    q = softmax_rows(f64(logits))
    qm = q.reshape(V // P, P, S)[::-1].reshape(V, S)
    nq = -q
    return np.abs(qm[:, idx] + nq)

@@ -1,0 +1,58 @@
+import concourse.mybir as mybir
+
+P = 128
+BLOCKS = 2
+CLASSES = 256
+LIST = 256
+PER_COLUMN = 16
+
+F32 = mybir.dt.float32
+U16 = mybir.dt.uint16
+ACT = mybir.ActivationFunctionType
+ADD = mybir.AluOpType.add
+ROW = mybir.AxisListType.X
+
+
+def tile_ageconditionedgraphpriorloss_kernel(tc, logits, offs, out):
+    nc = tc.nc
+    logits_blocks = logits.rearrange("(b p) s -> b p s", p=P)
+    out_blocks = out.rearrange("(b p) j -> b p j", p=P)
+
+    with tc.tile_pool(name="held", bufs=1) as held:
+        queues = [nc.sync, nc.scalar]
+
+        raw = []
+        for b in range(BLOCKS):
+            raw.append(held.tile([P, CLASSES], F32, name=f"raw{b}"))
+            queues[b].dma_start(raw[b][:], logits_blocks[b])
+
+        offsets = held.tile([P, LIST // PER_COLUMN], U16, name="offsets")
+        nc.sync.dma_start(offsets[:], offs)
+
+        q = []
+        nq = []
+        for b in range(BLOCKS):
+            neg_max = held.tile([P, 1], F32, name=f"neg_max{b}")
+            nc.vector.reduce_max(neg_max[:], raw[b][:], axis=ROW, negate=True)
+
+            expd = held.tile([P, CLASSES], F32, name=f"expd{b}")
+            total = held.tile([P, 1], F32, name=f"total{b}")
+            nc.scalar.activation(expd[:], raw[b][:], ACT.Exp, bias=neg_max[:], accum_out=total[:])
+
+            inv_total = held.tile([P, 1], F32, name=f"inv_total{b}")
+            nc.vector.reciprocal(inv_total[:], total[:])
+
+            q.append(held.tile([P, CLASSES], F32, name=f"q{b}"))
+            nc.vector.tensor_scalar_mul(q[b][:], expd[:], inv_total[:])
+
+            nq.append(held.tile([P, CLASSES], F32, name=f"nq{b}"))
+            nc.scalar.mul(nq[b][:], q[b][:], -1.0)
+
+        for b in range(BLOCKS):
+            mirror = BLOCKS - 1 - b
+            diff = held.tile([P, LIST], F32, name=f"diff{b}")
+            nc.vector.tensor_tensor(diff[:], q[mirror][:].indirect(offsets[:]), nq[b][:], ADD)
+
+            result = held.tile([P, LIST], F32, name=f"result{b}")
+            nc.scalar.activation(result[:], diff[:], ACT.Abs)
+            queues[b].dma_start(out_blocks[b], result[:])

@@ -29,6 +29,11 @@ def tile_ageconditionedgraphpriorloss_kernel(tc, logits, offs, out):
         offsets = held.tile([P, LIST // PER_COLUMN], U16, name="offsets")
         nc.sync.dma_start(offsets[:], offs)
 
+        zeros = held.tile([P, 1], F32, name="zeros")
+        nc.vector.memset(zeros[:], 0.0)
+        warmed = held.tile([P, 1], F32, name="warmed")
+        nc.scalar.activation(warmed[:], zeros[:], ACT.Exp)
+
         q = []
         nq = []
         for b in range(BLOCKS):

@@ -10,6 +10,8 @@ F32 = mybir.dt.float32
 U16 = mybir.dt.uint16
 ACT = mybir.ActivationFunctionType
 ADD = mybir.AluOpType.add
+MULT = mybir.AluOpType.mult
+MAX = mybir.AluOpType.max
 ROW = mybir.AxisListType.X
 
 
@@ -59,5 +61,8 @@ def tile_ageconditionedgraphpriorloss_kernel(tc, logits, offs, out):
             nc.vector.tensor_tensor(diff[:], q[mirror][:].indirect(offsets[:]), nq[b][:], ADD)
 
             result = held.tile([P, LIST], F32, name=f"result{b}")
-            nc.scalar.activation(result[:], diff[:], ACT.Abs)
+            if b < BLOCKS - 1:
+                nc.scalar.activation(result[:], diff[:], ACT.Abs)
+            else:
+                nc.vector.scalar_tensor_tensor(result[:], diff[:], -1.0, diff[:], op0=MULT, op1=MAX)
             queues[b].dma_start(out_blocks[b], result[:])

@@ -5,13 +5,12 @@ BLOCKS = 2
 CLASSES = 256
 LIST = 256
 PER_COLUMN = 16
+PIECE = 128
 
 F32 = mybir.dt.float32
 U16 = mybir.dt.uint16
 ACT = mybir.ActivationFunctionType
 ADD = mybir.AluOpType.add
-MULT = mybir.AluOpType.mult
-MAX = mybir.AluOpType.max
 ROW = mybir.AxisListType.X
 
 
@@ -58,11 +57,10 @@ def tile_ageconditionedgraphpriorloss_kernel(tc, logits, offs, out):
         for b in range(BLOCKS):
             mirror = BLOCKS - 1 - b
             diff = held.tile([P, LIST], F32, name=f"diff{b}")
-            nc.vector.tensor_tensor(diff[:], q[mirror][:].indirect(offsets[:]), nq[b][:], ADD)
-
             result = held.tile([P, LIST], F32, name=f"result{b}")
-            if b < BLOCKS - 1:
-                nc.scalar.activation(result[:], diff[:], ACT.Abs)
-            else:
-                nc.vector.scalar_tensor_tensor(result[:], diff[:], -1.0, diff[:], op0=MULT, op1=MAX)
-            queues[b].dma_start(out_blocks[b], result[:])
+            for i in range(LIST // PIECE):
+                columns = slice(i * PIECE, (i + 1) * PIECE)
+                entries = offsets[:, i * PIECE // PER_COLUMN : (i + 1) * PIECE // PER_COLUMN]
+                nc.vector.tensor_tensor(diff[:, columns], q[mirror][:].indirect(entries), nq[b][:, columns], ADD)
+                nc.scalar.activation(result[:, columns], diff[:, columns], ACT.Abs)
+                queues[i % len(queues)].dma_start(out_blocks[b][:, columns], result[:, columns])

@@ -5,7 +5,6 @@ BLOCKS = 2
 CLASSES = 256
 LIST = 256
 PER_COLUMN = 16
-PIECE = 128
 
 F32 = mybir.dt.float32
 U16 = mybir.dt.uint16
@@ -20,12 +19,10 @@ def tile_ageconditionedgraphpriorloss_kernel(tc, logits, offs, out):
     out_blocks = out.rearrange("(b p) j -> b p j", p=P)
 
     with tc.tile_pool(name="held", bufs=1) as held:
-        queues = [nc.sync, nc.scalar]
-
         raw = []
         for b in range(BLOCKS):
             raw.append(held.tile([P, CLASSES], F32, name=f"raw{b}"))
-            queues[b].dma_start(raw[b][:], logits_blocks[b])
+            nc.sync.dma_start(raw[b][:], logits_blocks[b])
 
         offsets = held.tile([P, LIST // PER_COLUMN], U16, name="offsets")
         nc.sync.dma_start(offsets[:], offs)
@@ -54,13 +51,12 @@ def tile_ageconditionedgraphpriorloss_kernel(tc, logits, offs, out):
             nq.append(held.tile([P, CLASSES], F32, name=f"nq{b}"))
             nc.scalar.mul(nq[b][:], q[b][:], -1.0)
 
+        queues = [nc.sync, nc.scalar]
         for b in range(BLOCKS):
             mirror = BLOCKS - 1 - b
             diff = held.tile([P, LIST], F32, name=f"diff{b}")
+            nc.vector.tensor_tensor(diff[:], q[mirror][:].indirect(offsets[:]), nq[b][:], ADD)
+
             result = held.tile([P, LIST], F32, name=f"result{b}")
-            for i in range(LIST // PIECE):
-                columns = slice(i * PIECE, (i + 1) * PIECE)
-                entries = offsets[:, i * PIECE // PER_COLUMN : (i + 1) * PIECE // PER_COLUMN]
-                nc.vector.tensor_tensor(diff[:, columns], q[mirror][:].indirect(entries), nq[b][:, columns], ADD)
-                nc.scalar.activation(result[:, columns], diff[:, columns], ACT.Abs)
-                queues[i % len(queues)].dma_start(out_blocks[b][:, columns], result[:, columns])
+            nc.scalar.activation(result[:], diff[:], ACT.Abs)
+            queues[b].dma_start(out_blocks[b], result[:])

@@ -51,7 +51,6 @@ def tile_ageconditionedgraphpriorloss_kernel(tc, logits, offs, out):
             nq.append(held.tile([P, CLASSES], F32, name=f"nq{b}"))
             nc.scalar.mul(nq[b][:], q[b][:], -1.0)
 
-        queues = [nc.sync, nc.scalar]
         for b in range(BLOCKS):
             mirror = BLOCKS - 1 - b
             diff = held.tile([P, LIST], F32, name=f"diff{b}")
@@ -59,4 +58,4 @@ def tile_ageconditionedgraphpriorloss_kernel(tc, logits, offs, out):
 
             result = held.tile([P, LIST], F32, name=f"result{b}")
             nc.scalar.activation(result[:], diff[:], ACT.Abs)
-            queues[b].dma_start(out_blocks[b], result[:])
+            nc.sync.dma_start(out_blocks[b], result[:])

@@ -5,6 +5,7 @@ BLOCKS = 2
 CLASSES = 256
 LIST = 256
 PER_COLUMN = 16
+PIECE = 128
 
 F32 = mybir.dt.float32
 U16 = mybir.dt.uint16
@@ -32,30 +33,39 @@ def tile_ageconditionedgraphpriorloss_kernel(tc, logits, offs, out):
         warmed = held.tile([P, 1], F32, name="warmed")
         nc.scalar.activation(warmed[:], zeros[:], ACT.Exp)
 
+        neg_max = []
+        for b in range(BLOCKS):
+            neg_max.append(held.tile([P, 1], F32, name=f"neg_max{b}"))
+            nc.vector.reduce_max(neg_max[b][:], raw[b][:], axis=ROW, negate=True)
+
+        expd = []
+        total = []
+        for b in range(BLOCKS):
+            expd.append(held.tile([P, CLASSES], F32, name=f"expd{b}"))
+            total.append(held.tile([P, 1], F32, name=f"total{b}"))
+            nc.scalar.activation(expd[b][:], raw[b][:], ACT.Exp, bias=neg_max[b][:], accum_out=total[b][:])
+
         q = []
         nq = []
         for b in range(BLOCKS):
-            neg_max = held.tile([P, 1], F32, name=f"neg_max{b}")
-            nc.vector.reduce_max(neg_max[:], raw[b][:], axis=ROW, negate=True)
-
-            expd = held.tile([P, CLASSES], F32, name=f"expd{b}")
-            total = held.tile([P, 1], F32, name=f"total{b}")
-            nc.scalar.activation(expd[:], raw[b][:], ACT.Exp, bias=neg_max[:], accum_out=total[:])
-
             inv_total = held.tile([P, 1], F32, name=f"inv_total{b}")
-            nc.vector.reciprocal(inv_total[:], total[:])
+            nc.vector.reciprocal(inv_total[:], total[b][:])
 
             q.append(held.tile([P, CLASSES], F32, name=f"q{b}"))
-            nc.vector.tensor_scalar_mul(q[b][:], expd[:], inv_total[:])
+            nc.vector.tensor_scalar_mul(q[b][:], expd[b][:], inv_total[:])
 
             nq.append(held.tile([P, CLASSES], F32, name=f"nq{b}"))
             nc.scalar.mul(nq[b][:], q[b][:], -1.0)
 
         for b in range(BLOCKS):
             mirror = BLOCKS - 1 - b
-            diff = held.tile([P, LIST], F32, name=f"diff{b}")
-            nc.vector.tensor_tensor(diff[:], q[mirror][:].indirect(offsets[:]), nq[b][:], ADD)
+            for first in range(0, LIST, PIECE):
+                piece_offsets = offsets[:, first // PER_COLUMN : (first + PIECE) // PER_COLUMN]
+                diff = held.tile([P, PIECE], F32, name=f"diff{b}_{first}")
+                nc.vector.tensor_tensor(
+                    diff[:], q[mirror][:].indirect(piece_offsets), nq[b][:, first : first + PIECE], ADD
+                )
 
-            result = held.tile([P, LIST], F32, name=f"result{b}")
-            nc.scalar.activation(result[:], diff[:], ACT.Abs)
-            nc.sync.dma_start(out_blocks[b], result[:])
+                result = held.tile([P, PIECE], F32, name=f"result{b}_{first}")
+                nc.scalar.activation(result[:], diff[:], ACT.Abs)
+                nc.sync.dma_start(out_blocks[b][:, first : first + PIECE], result[:])

@@ -5,7 +5,6 @@ BLOCKS = 2
 CLASSES = 256
 LIST = 256
 PER_COLUMN = 16
-PIECE = 128
 
 F32 = mybir.dt.float32
 U16 = mybir.dt.uint16
@@ -59,13 +58,14 @@ def tile_ageconditionedgraphpriorloss_kernel(tc, logits, offs, out):
 
         for b in range(BLOCKS):
             mirror = BLOCKS - 1 - b
-            for first in range(0, LIST, PIECE):
-                piece_offsets = offsets[:, first // PER_COLUMN : (first + PIECE) // PER_COLUMN]
-                diff = held.tile([P, PIECE], F32, name=f"diff{b}_{first}")
+            piece = LIST if b < BLOCKS - 1 else LIST // 2
+            for first in range(0, LIST, piece):
+                piece_offsets = offsets[:, first // PER_COLUMN : (first + piece) // PER_COLUMN]
+                diff = held.tile([P, piece], F32, name=f"diff{b}_{first}")
                 nc.vector.tensor_tensor(
-                    diff[:], q[mirror][:].indirect(piece_offsets), nq[b][:, first : first + PIECE], ADD
+                    diff[:], q[mirror][:].indirect(piece_offsets), nq[b][:, first : first + piece], ADD
                 )
 
-                result = held.tile([P, PIECE], F32, name=f"result{b}_{first}")
+                result = held.tile([P, piece], F32, name=f"result{b}_{first}")
                 nc.scalar.activation(result[:], diff[:], ACT.Abs)
-                nc.sync.dma_start(out_blocks[b][:, first : first + PIECE], result[:])
+                nc.sync.dma_start(out_blocks[b][:, first : first + piece], result[:])

@@ -8,6 +8,8 @@ PER_COLUMN = 16
 
 F32 = mybir.dt.float32
 U16 = mybir.dt.uint16
+I32 = mybir.dt.int32
+ALL_BUT_SIGN = 0x7FFFFFFF
 ACT = mybir.ActivationFunctionType
 ADD = mybir.AluOpType.add
 ROW = mybir.AxisListType.X
@@ -67,5 +69,10 @@ def tile_ageconditionedgraphpriorloss_kernel(tc, logits, offs, out):
                 )
 
                 result = held.tile([P, piece], F32, name=f"result{b}_{first}")
-                nc.scalar.activation(result[:], diff[:], ACT.Abs)
+                if b == BLOCKS - 1 and first + piece == LIST:
+                    nc.vector.tensor_single_scalar(
+                        result[:].bitcast(I32), diff[:].bitcast(I32), ALL_BUT_SIGN, op=mybir.AluOpType.bitwise_and
+                    )
+                else:
+                    nc.scalar.activation(result[:], diff[:], ACT.Abs)
                 nc.sync.dma_start(out_blocks[b][:, first : first + piece], result[:])

@@ -56,7 +56,10 @@ def tile_ageconditionedgraphpriorloss_kernel(tc, logits, offs, out):
             nc.vector.tensor_scalar_mul(q[b][:], expd[b][:], inv_total[:])
 
             nq.append(held.tile([P, CLASSES], F32, name=f"nq{b}"))
-            nc.scalar.mul(nq[b][:], q[b][:], -1.0)
+            if b == 0:
+                nc.vector.tensor_scalar_mul(nq[b][:], q[b][:], -1.0)
+            else:
+                nc.scalar.mul(nq[b][:], q[b][:], -1.0)
 
         for b in range(BLOCKS):
             mirror = BLOCKS - 1 - b

@@ -46,20 +46,21 @@ def tile_ageconditionedgraphpriorloss_kernel(tc, logits, offs, out):
             total.append(held.tile([P, 1], F32, name=f"total{b}"))
             nc.scalar.activation(expd[b][:], raw[b][:], ACT.Exp, bias=neg_max[b][:], accum_out=total[b][:])
 
-        q = []
-        nq = []
+        neg_expd0 = held.tile([P, CLASSES], F32, name="neg_expd0")
+        nc.vector.tensor_scalar_mul(neg_expd0[:], expd[0][:], -1.0)
+
+        inv_total = []
         for b in range(BLOCKS):
-            inv_total = held.tile([P, 1], F32, name=f"inv_total{b}")
-            nc.vector.reciprocal(inv_total[:], total[b][:])
+            inv_total.append(held.tile([P, 1], F32, name=f"inv_total{b}"))
+            nc.vector.reciprocal(inv_total[b][:], total[b][:])
 
-            q.append(held.tile([P, CLASSES], F32, name=f"q{b}"))
-            nc.vector.tensor_scalar_mul(q[b][:], expd[b][:], inv_total[:])
+        q = [held.tile([P, CLASSES], F32, name=f"q{b}") for b in range(BLOCKS)]
+        nq = [held.tile([P, CLASSES], F32, name=f"nq{b}") for b in range(BLOCKS)]
 
-            nq.append(held.tile([P, CLASSES], F32, name=f"nq{b}"))
-            if b == 0:
-                nc.vector.tensor_scalar_mul(nq[b][:], q[b][:], -1.0)
-            else:
-                nc.scalar.mul(nq[b][:], q[b][:], -1.0)
+        nc.scalar.mul(nq[0][:], neg_expd0[:], inv_total[0][:])
+        nc.scalar.mul(q[0][:], expd[0][:], inv_total[0][:])
+        nc.vector.tensor_scalar_mul(q[1][:], expd[1][:], inv_total[1][:])
+        nc.scalar.mul(nq[1][:], q[1][:], -1.0)
 
         for b in range(BLOCKS):
             mirror = BLOCKS - 1 - b

@@ -29,10 +29,19 @@ def tile_ageconditionedgraphpriorloss_kernel(tc, logits, offs, out):
         offsets = held.tile([P, LIST // PER_COLUMN], U16, name="offsets")
         nc.sync.dma_start(offsets[:], offs)
 
-        zeros = held.tile([P, 1], F32, name="zeros")
-        nc.vector.memset(zeros[:], 0.0)
-        warmed = held.tile([P, 1], F32, name="warmed")
-        nc.scalar.activation(warmed[:], zeros[:], ACT.Exp)
+        ones = held.tile([P, 1], F32, name="ones")
+        nc.vector.memset(ones[:], 1.0)
+        warm = [held.tile([P, 1], F32, name=f"warm{k}") for k in range(9)]
+        nc.scalar.activation(warm[0][:], ones[:], ACT.Exp, bias=ones[:], accum_out=warm[1][:])
+        nc.scalar.mul(warm[2][:], ones[:], ones[:])
+        nc.scalar.activation(warm[3][:], ones[:], ACT.Abs)
+        nc.vector.reduce_max(warm[4][:], ones[:], axis=ROW, negate=True)
+        nc.vector.reciprocal(warm[5][:], ones[:])
+        nc.vector.tensor_scalar_mul(warm[6][:], ones[:], ones[:])
+        nc.vector.tensor_tensor(warm[7][:], ones[:], ones[:], ADD)
+        nc.vector.tensor_single_scalar(
+            warm[8][:].bitcast(I32), ones[:].bitcast(I32), ALL_BUT_SIGN, op=mybir.AluOpType.bitwise_and
+        )
 
         neg_max = []
         for b in range(BLOCKS):

import concourse.mybir as mybir

P = 128
BLOCKS = 2
CLASSES = 256
LIST = 256
PER_COLUMN = 16

F32 = mybir.dt.float32
U16 = mybir.dt.uint16
I32 = mybir.dt.int32
ALL_BUT_SIGN = 0x7FFFFFFF
ACT = mybir.ActivationFunctionType
ADD = mybir.AluOpType.add
ROW = mybir.AxisListType.X


def tile_ageconditionedgraphpriorloss_kernel(tc, logits, offs, out):
    nc = tc.nc
    logits_blocks = logits.rearrange("(b p) s -> b p s", p=P)
    out_blocks = out.rearrange("(b p) j -> b p j", p=P)

    with tc.tile_pool(name="held", bufs=1) as held:
        raw = []
        for b in range(BLOCKS):
            raw.append(held.tile([P, CLASSES], F32, name=f"raw{b}"))
            nc.sync.dma_start(raw[b][:], logits_blocks[b])

        offsets = held.tile([P, LIST // PER_COLUMN], U16, name="offsets")
        nc.sync.dma_start(offsets[:], offs)

        ones = held.tile([P, 1], F32, name="ones")
        nc.vector.memset(ones[:], 1.0)
        warm = [held.tile([P, 1], F32, name=f"warm{k}") for k in range(9)]
        nc.scalar.activation(warm[0][:], ones[:], ACT.Exp, bias=ones[:], accum_out=warm[1][:])
        nc.scalar.mul(warm[2][:], ones[:], ones[:])
        nc.scalar.activation(warm[3][:], ones[:], ACT.Abs)
        nc.vector.reduce_max(warm[4][:], ones[:], axis=ROW, negate=True)
        nc.vector.reciprocal(warm[5][:], ones[:])
        nc.vector.tensor_scalar_mul(warm[6][:], ones[:], ones[:])
        nc.vector.tensor_tensor(warm[7][:], ones[:], ones[:], ADD)
        nc.vector.tensor_single_scalar(
            warm[8][:].bitcast(I32), ones[:].bitcast(I32), ALL_BUT_SIGN, op=mybir.AluOpType.bitwise_and
        )

        neg_max = []
        for b in range(BLOCKS):
            neg_max.append(held.tile([P, 1], F32, name=f"neg_max{b}"))
            nc.vector.reduce_max(neg_max[b][:], raw[b][:], axis=ROW, negate=True)

        expd = []
        total = []
        for b in range(BLOCKS):
            expd.append(held.tile([P, CLASSES], F32, name=f"expd{b}"))
            total.append(held.tile([P, 1], F32, name=f"total{b}"))
            nc.scalar.activation(expd[b][:], raw[b][:], ACT.Exp, bias=neg_max[b][:], accum_out=total[b][:])

        neg_expd0 = held.tile([P, CLASSES], F32, name="neg_expd0")
        nc.vector.tensor_scalar_mul(neg_expd0[:], expd[0][:], -1.0)

        inv_total = []
        for b in range(BLOCKS):
            inv_total.append(held.tile([P, 1], F32, name=f"inv_total{b}"))
            nc.vector.reciprocal(inv_total[b][:], total[b][:])

        q = [held.tile([P, CLASSES], F32, name=f"q{b}") for b in range(BLOCKS)]
        nq = [held.tile([P, CLASSES], F32, name=f"nq{b}") for b in range(BLOCKS)]

        nc.scalar.mul(nq[0][:], neg_expd0[:], inv_total[0][:])
        nc.scalar.mul(q[0][:], expd[0][:], inv_total[0][:])
        nc.vector.tensor_scalar_mul(q[1][:], expd[1][:], inv_total[1][:])
        nc.scalar.mul(nq[1][:], q[1][:], -1.0)

        for b in range(BLOCKS):
            mirror = BLOCKS - 1 - b
            piece = LIST if b < BLOCKS - 1 else LIST // 2
            for first in range(0, LIST, piece):
                piece_offsets = offsets[:, first // PER_COLUMN : (first + piece) // PER_COLUMN]
                diff = held.tile([P, piece], F32, name=f"diff{b}_{first}")
                nc.vector.tensor_tensor(
                    diff[:], q[mirror][:].indirect(piece_offsets), nq[b][:, first : first + piece], ADD
                )

                result = held.tile([P, piece], F32, name=f"result{b}_{first}")
                if b == BLOCKS - 1 and first + piece == LIST:
                    nc.vector.tensor_single_scalar(
                        result[:].bitcast(I32), diff[:].bitcast(I32), ALL_BUT_SIGN, op=mybir.AluOpType.bitwise_and
                    )
                else:
                    nc.scalar.activation(result[:], diff[:], ACT.Abs)
                nc.sync.dma_start(out_blocks[b][:, first : first + piece], result[:])
